import numpy as np
import ml_dtypes


def mxq(x, axis, fmt="e4m3"):
    dtype, down = {"e4m3": (ml_dtypes.float8_e4m3fn, 7), "e5m2": (ml_dtypes.float8_e5m2, 14)}[fmt]
    v = np.moveaxis(np.asarray(x, np.float32).astype(ml_dtypes.bfloat16).astype(np.float64), axis, -1)
    blocks = v.reshape(v.shape[:-1] + (-1, 32))
    amax = np.abs(blocks).max(-1, keepdims=True)
    byte = np.maximum(np.where(amax > 0, np.frexp(amax)[1] - 1 + 127, 0) - down, 1)
    scale = np.exp2(byte - 127.0)
    codes = (blocks / scale).astype(np.float32).astype(dtype).astype(np.float64)
    return np.moveaxis((codes * scale).reshape(v.shape), -1, axis)


WIDE = False


def mx_kscale(k):
    if not WIDE:
        return np.ones(k)
    levels = np.array([10, -10, 5, -5, 0])
    a = np.random.permutation(np.resize(levels, k // 512 * 4)).reshape(k // 512, 4)
    idx = np.arange(k)
    return np.exp2(a[idx // 512, idx % 128 // 32])


BF16 = ml_dtypes.bfloat16


def bf(x):
    return np.asarray(x, np.float32).astype(BF16)


def f64(x):
    return np.asarray(x).astype(np.float64)


B, S, D, H, DH, DR, DKV, DQ = 1, 1024, 2048, 16, 128, 64, 512, 1024
HALF = DR // 2


def rope(t, cos, sin):
    t1, t2 = t[..., 0::2], t[..., 1::2]
    c = cos[None, :, None, :]
    s = sin[None, :, None, :]
    return np.stack([t1 * c - t2 * s, t1 * s + t2 * c], axis=-1).reshape(t.shape)


def setup_inputs():
    s, t = mx_kscale(D), mx_kscale(DQ)
    ang = np.random.uniform(0.0, 2.0 * np.pi, (S, HALF))
    return {"x": bf(np.random.standard_normal((B, S, D)) * s),
            "W_q_down": bf(np.random.standard_normal((D, DQ)) / np.sqrt(D) / s[:, None] * t),
            "W_q_up": bf(np.random.standard_normal((DQ, H * DH)) / np.sqrt(DQ) / t[:, None]),
            "W_q_rope": bf(np.random.standard_normal((DQ, H * DR)) / np.sqrt(DQ) / t[:, None]),
            "rope_cos": bf(np.cos(ang)), "rope_sin": bf(np.sin(ang))}


def reference(x, W_q_down, W_q_up, W_q_rope, rope_cos, rope_sin):
    down_q = mxq(f64(x), 2, "e4m3") @ mxq(f64(W_q_down), 0, "e4m3")
    dq = mxq(down_q, 2, "e4m3")
    q_c = (dq @ mxq(f64(W_q_up), 0, "e4m3")).reshape(B, S, H, DH)
    q_r = (dq @ mxq(f64(W_q_rope), 0, "e4m3")).reshape(B, S, H, DR)
    q_r = rope(q_r, f64(rope_cos), f64(rope_sin))
    return np.concatenate([q_c, q_r], axis=-1).transpose(0, 2, 1, 3)

@@ -1,0 +1,293 @@
+from concourse import mybir
+from concourse.masks import make_identity
+
+BF16 = mybir.dt.bfloat16
+F32 = mybir.dt.float32
+U32 = mybir.dt.uint32
+U8 = mybir.dt.uint8
+FP8X4 = mybir.dt.float8_e4m3fn_x4
+MULT = mybir.AluOpType.mult
+ADD = mybir.AluOpType.add
+
+P = 128
+PACK = 4
+K_PASS = P * PACK
+BANK = 512
+
+S, D, DQ = 1024, 2048, 1024
+H, DH, DR = 16, 128, 64
+HALF = DR // 2
+J = S // P
+PAIRS = J // 2
+D_PASSES = D // K_PASS
+DQ_PASSES = DQ // K_PASS
+GROUP_HEADS = BANK // DH
+GROUPS = H // GROUP_HEADS
+ROPE_COLS = GROUP_HEADS * DR
+QUAD = 4
+
+VECTOR_COLS = 320
+
+FLOPS = 2 * S * D * DQ + 2 * S * DQ * (H * DH + H * DR)
+
+
+def tile_multiheadlatentattention_pa_kernel(
+    tc, x, w_down, w_up, w_rope, rope_cos, rope_sin, out
+):
+    nc = tc.nc
+    x_rows = x.flatten_outer_dims().rearrange("(p j) d -> p j d", j=J)
+    out_rows = out.flatten_outer_dims().rearrange("(h p j) f -> p h j f", h=H, j=J)
+
+    with tc.tile_pool(name="const", bufs=1) as const, tc.tile_pool(
+        name="raw8", bufs=5
+    ) as raw8, tc.tile_pool(name="raw4", bufs=2 * D_PASSES) as raw4, tc.tile_pool(
+        name="wgroup", bufs=3
+    ) as wgroup, tc.tile_pool(name="agroup", bufs=2) as agroup, tc.tile_pool(
+        name="xq", bufs=J
+    ) as xq, tc.tile_pool(name="wdq", bufs=2 * D_PASSES) as wdq, tc.tile_pool(
+        name="dqq", bufs=DQ_PASSES * PAIRS
+    ) as dqq, tc.tile_pool(name="w2q", bufs=12) as w2q, tc.tile_pool(
+        name="parts", bufs=3
+    ) as parts, tc.tile_pool(name="outs", bufs=3) as outs, tc.psum_pool(
+        name="psum", bufs=8
+    ) as psum:
+        ident = const.tile([P, P], F32)
+        make_identity(nc, ident[:])
+        cos_sb = const.tile([P, J, HALF], BF16)
+        sin_sb = const.tile([P, J, HALF], BF16)
+        nc.scalar.dma_start(out=cos_sb[:], in_=rope_cos.rearrange("(p j) i -> p j i", j=J))
+        nc.scalar.dma_start(out=sin_sb[:], in_=rope_sin.rearrange("(p j) i -> p j i", j=J))
+        even_factor = const.tile([P, J, HALF, 2], F32)
+        odd_factor = const.tile([P, J, HALF, 2], F32)
+        nc.gpsimd.tensor_copy(out=even_factor[:, :, :, 0], in_=cos_sb[:])
+        nc.gpsimd.tensor_copy(out=even_factor[:, :, :, 1], in_=sin_sb[:])
+        nc.gpsimd.tensor_scalar(
+            out=odd_factor[:, :, :, 0], in0=sin_sb[:], scalar1=-1.0, scalar2=0.0, op0=MULT, op1=ADD
+        )
+        nc.gpsimd.tensor_copy(out=odd_factor[:, :, :, 1], in_=cos_sb[:])
+
+        x_raw = {}
+        wd_raw = {}
+        w2_raw = {}
+        x_codes = {}
+        wd_codes = {}
+        dq_codes = {}
+        w2_codes = {}
+
+        def load_x(pair):
+            t = raw8.tile([P, 2 * D], BF16, tag="raw8", name="x_raw")
+            nc.sync.dma_start(
+                out=t[:].rearrange("p (j d) -> p j d", j=2), in_=x_rows[:, 2 * pair : 2 * pair + 2, :]
+            )
+            x_raw[pair] = t
+
+        def load_w_down(half):
+            cols = slice(half * BANK, (half + 1) * BANK)
+            for c in range(D_PASSES):
+                t = raw4.tile([P, PACK, BANK], BF16, tag="raw4", name="wd_raw")
+                for u in range(2):
+                    row0 = c * K_PASS + u * 2 * P
+                    nc.sync.dma_start(
+                        out=t[:, 2 * u : 2 * u + 2, :],
+                        in_=w_down[row0 : row0 + 2 * P, cols].rearrange("(q e) n -> q e n", e=2),
+                    )
+                wd_raw[(c, half)] = t
+
+        def load_stage2(key):
+            name, g, half = key
+            src = w_up[:, half * 2 * BANK : (half + 1) * 2 * BANK] if name == "up" else w_rope
+            t = raw8.tile([P, PACK, 2 * BANK], BF16, tag="raw8", name="w2_raw")
+            nc.sync.dma_start(
+                out=t[:], in_=src[g * K_PASS : (g + 1) * K_PASS, :].rearrange("(t p) n -> p t n", p=P)
+            )
+            w2_raw[key] = t
+
+        stage2_order = []
+        for half in range(2):
+            for g in range(DQ_PASSES):
+                stage2_order.append(("up", g, half))
+            if half == 0:
+                for g in range(DQ_PASSES):
+                    stage2_order.append(("rope", g, 0))
+
+        def quantise_weight_block(pool, rows):
+            grouped = wgroup.tile([P, BANK, PACK], BF16, align_bytes=64, tag="wg", name="grouped")
+            v = VECTOR_COLS
+            nc.vector.tensor_copy(
+                out=grouped[:, 0:v, :].rearrange("p (c i) t -> p c t i", i=4),
+                in_=rows[:, :, 0:v].rearrange("p t (c i) -> p c t i", i=4),
+            )
+            nc.scalar.copy(
+                out=grouped[:, v:BANK, :].rearrange("p (c i) t -> p c t i", i=4),
+                in_=rows[:, :, v:BANK].rearrange("p t (c i) -> p c t i", i=4),
+            )
+            codes = pool.tile([P, BANK], U32, align_bytes=64, tag="codes", name="codes")
+            scales = pool.tile([P, BANK], U8, align_bytes=64, tag="scales", name="scales")
+            nc.vector.quantize_mx(
+                out=codes[:].bitcast(FP8X4),
+                scales=scales[:],
+                in_=grouped[:].rearrange("p n t -> p (n t)"),
+            )
+            return codes, scales
+
+        def x_to_codes(pair):
+            words = x_raw[pair][:].bitcast(F32)
+            for jl in range(2):
+                grouped = agroup.tile([P, D], BF16, align_bytes=64, tag="xg", name="x_grouped")
+                grouped_words = grouped[:].bitcast(F32).rearrange(
+                    "q (c s u) -> q c s u", c=D_PASSES, u=2
+                )
+                for b in range(2):
+                    xt = psum.tile([P, BANK], F32, tag="bank", name="xt")
+                    for cl in range(2):
+                        for u in range(2):
+                            col0 = jl * (D // 2) + (2 * b + cl) * 2 * P + u * P
+                            nc.tensor.transpose(
+                                xt[:, (2 * cl + u) * P : (2 * cl + u + 1) * P],
+                                words[:, col0 : col0 + P],
+                                ident[:],
+                            )
+                    nc.scalar.copy(
+                        out=grouped_words[:, 2 * b : 2 * b + 2, :, :],
+                        in_=xt[:].rearrange("q (c u s) -> q c s u", c=2, u=2),
+                    )
+                codes = xq.tile([P, D_PASSES * P], U32, align_bytes=64, tag="codes", name="x_codes")
+                scales = xq.tile([P, D_PASSES * P], U8, align_bytes=64, tag="scales", name="x_scales")
+                nc.vector.quantize_mx(out=codes[:].bitcast(FP8X4), scales=scales[:], in_=grouped[:])
+                x_codes[2 * pair + jl] = (codes, scales)
+
+        def down_projection(half, pair):
+            grouped = agroup.tile([P, 2, P, PACK], BF16, align_bytes=64, tag="dqg", name="dq_grouped")
+            for jl in range(2):
+                xc, xs = x_codes[2 * pair + jl]
+                acc = psum.tile([P, BANK], F32, tag="bank", name="dq_acc")
+                for t in range(PACK):
+                    for c in range(D_PASSES):
+                        wc, ws = wd_codes[(c, half)]
+                        nc.tensor.matmul_mx(
+                            out=acc[:, t * P : (t + 1) * P],
+                            lhsT=wc[:, t * P : (t + 1) * P].bitcast(FP8X4),
+                            lhsT_scale=ws[:, t * P : (t + 1) * P],
+                            rhs=xc[:, c * P : (c + 1) * P].bitcast(FP8X4),
+                            rhs_scale=xs[:, c * P : (c + 1) * P],
+                            start=(c == 0),
+                            stop=(c == D_PASSES - 1),
+                        )
+                nc.scalar.copy(
+                    out=grouped[:, jl, :, :], in_=acc[:].rearrange("p (t s) -> p s t", t=PACK)
+                )
+            codes = dqq.tile([P, 2 * P], U32, align_bytes=64, tag="codes", name="dq_codes")
+            scales = dqq.tile([P, 2 * P], U8, align_bytes=64, tag="scales", name="dq_scales")
+            nc.vector.quantize_mx(
+                out=codes[:].bitcast(FP8X4),
+                scales=scales[:],
+                in_=grouped[:].rearrange("p j s t -> p (j s t)"),
+            )
+            dq_codes[(half, pair)] = (codes, scales)
+
+        def quantise_group_weights(group):
+            half, side = group // 2, group % 2
+            for g in range(DQ_PASSES):
+                w2_codes[("up", g, group)] = quantise_weight_block(
+                    w2q, w2_raw[("up", g, half)][:, :, side * BANK : (side + 1) * BANK]
+                )
+            if side == 0:
+                for g in range(DQ_PASSES):
+                    w2_codes[("rope", g, half)] = quantise_weight_block(
+                        w2q, w2_raw[("rope", g, 0)][:, :, half * BANK : (half + 1) * BANK]
+                    )
+
+        def up_projection(acc, j, weights, col0, width):
+            for g in range(DQ_PASSES):
+                ac, asc = dq_codes[(g, j // 2)]
+                wc, ws = weights[g]
+                tok = slice((j % 2) * P, (j % 2 + 1) * P)
+                nc.tensor.matmul_mx(
+                    out=acc,
+                    lhsT=ac[:, tok].bitcast(FP8X4),
+                    lhsT_scale=asc[:, tok],
+                    rhs=wc[:, col0 : col0 + width].bitcast(FP8X4),
+                    rhs_scale=ws[:, col0 : col0 + width],
+                    start=(g == 0),
+                    stop=(g == DQ_PASSES - 1),
+                )
+
+        def head_group(group):
+            up_w = [w2_codes[("up", g, group)] for g in range(DQ_PASSES)]
+            rope_w = [w2_codes[("rope", g, group // 2)] for g in range(DQ_PASSES)]
+            shape = [P, 2, GROUP_HEADS, HALF, 2]
+            for quad in range(J // QUAD):
+                result = outs.tile([P, GROUP_HEADS, QUAD, DH + DR], F32, tag="res", name="result")
+                for jp in range(QUAD // 2):
+                    j0 = quad * QUAD + 2 * jp
+                    qr = psum.tile([P, BANK], F32, tag="bank", name="qr")
+                    for jl in range(2):
+                        qc = psum.tile([P, BANK], F32, tag="bank", name="qc")
+                        up_projection(qc[:], j0 + jl, up_w, 0, BANK)
+                        nc.scalar.copy(
+                            out=result[:, :, 2 * jp + jl, 0:DH],
+                            in_=qc[:].rearrange("p (h d) -> p h d", h=GROUP_HEADS),
+                        )
+                    for jl in range(2):
+                        up_projection(
+                            qr[:, jl * ROPE_COLS : (jl + 1) * ROPE_COLS],
+                            j0 + jl,
+                            rope_w,
+                            (group % 2) * ROPE_COLS,
+                            ROPE_COLS,
+                        )
+                    pairs = qr[:].rearrange("p (j h i e) -> p j h i e", j=2, h=GROUP_HEADS, e=2)
+                    even_part = parts.tile(shape, F32, tag="even", name="even_part")
+                    odd_part = parts.tile(shape, F32, tag="odd", name="odd_part")
+                    nc.vector.tensor_tensor(
+                        out=even_part[:],
+                        in0=pairs[:, :, :, :, 0:1].to_broadcast(shape),
+                        in1=even_factor[:, j0 : j0 + 2, :, :].unsqueeze(2).to_broadcast(shape),
+                        op=MULT,
+                    )
+                    nc.vector.tensor_tensor(
+                        out=odd_part[:],
+                        in0=pairs[:, :, :, :, 1:2].to_broadcast(shape),
+                        in1=odd_factor[:, j0 : j0 + 2, :, :].unsqueeze(2).to_broadcast(shape),
+                        op=MULT,
+                    )
+                    nc.gpsimd.tensor_tensor(
+                        out=result[:, :, 2 * jp : 2 * jp + 2, DH : DH + DR],
+                        in0=even_part[:].rearrange("p j h i e -> p h j (i e)"),
+                        in1=odd_part[:].rearrange("p j h i e -> p h j (i e)"),
+                        op=ADD,
+                    )
+                nc.sync.dma_start(
+                    out=out_rows[
+                        :,
+                        group * GROUP_HEADS : (group + 1) * GROUP_HEADS,
+                        quad * QUAD : (quad + 1) * QUAD,
+                        :,
+                    ],
+                    in_=result[:],
+                )
+
+        load_x(0)
+        load_w_down(0)
+        for pair in range(1, PAIRS):
+            load_x(pair)
+        load_w_down(1)
+        load_stage2(stage2_order[0])
+
+        x_to_codes(0)
+        load_stage2(stage2_order[1])
+        for c in range(D_PASSES):
+            wd_codes[(c, 0)] = quantise_weight_block(wdq, wd_raw[(c, 0)][:])
+        for pair in range(PAIRS):
+            if pair + 1 < PAIRS:
+                x_to_codes(pair + 1)
+                load_stage2(stage2_order[pair + 2])
+            down_projection(0, pair)
+            wd_codes[(pair, 1)] = quantise_weight_block(wdq, wd_raw[(pair, 1)][:])
+        for pair in range(PAIRS):
+            down_projection(1, pair)
+            quantise_group_weights(pair)
+            if pair == 1:
+                load_stage2(stage2_order[5])
+        for group in range(GROUPS):
+            head_group(group)

@@ -39,8 +39,8 @@ def tile_multiheadlatentattention_pa_kernel(
     out_rows = out.flatten_outer_dims().rearrange("(h p j) f -> p h j f", h=H, j=J)
 
     with tc.tile_pool(name="const", bufs=1) as const, tc.tile_pool(
-        name="raw8", bufs=5
-    ) as raw8, tc.tile_pool(name="raw4", bufs=2 * D_PASSES) as raw4, tc.tile_pool(
+        name="raw8", bufs=6
+    ) as raw8, tc.tile_pool(name="raw4", bufs=D_PASSES) as raw4, tc.tile_pool(
         name="wgroup", bufs=3
     ) as wgroup, tc.tile_pool(name="agroup", bufs=2) as agroup, tc.tile_pool(
         name="xq", bufs=J
@@ -185,17 +185,21 @@ def tile_multiheadlatentattention_pa_kernel(
             )
             dq_codes[(half, pair)] = (codes, scales)
 
-        def quantise_group_weights(group):
-            half, side = group // 2, group % 2
+        stage2_blocks = []
+        for group in range(GROUPS):
             for g in range(DQ_PASSES):
-                w2_codes[("up", g, group)] = quantise_weight_block(
-                    w2q, w2_raw[("up", g, half)][:, :, side * BANK : (side + 1) * BANK]
-                )
-            if side == 0:
+                stage2_blocks.append(("up", g, group))
+            if group % 2 == 0:
                 for g in range(DQ_PASSES):
-                    w2_codes[("rope", g, half)] = quantise_weight_block(
-                        w2q, w2_raw[("rope", g, 0)][:, :, half * BANK : (half + 1) * BANK]
-                    )
+                    stage2_blocks.append(("rope", g, group // 2))
+
+        def quantise_stage2_block(n):
+            name, g, part = stage2_blocks[n]
+            rows = w2_raw[("up", g, part // 2)] if name == "up" else w2_raw[("rope", g, 0)]
+            side = part % 2
+            w2_codes[stage2_blocks[n]] = quantise_weight_block(
+                w2q, rows[:, :, side * BANK : (side + 1) * BANK]
+            )
 
         def up_projection(acc, j, weights, col0, width):
             for g in range(DQ_PASSES):
@@ -216,18 +220,12 @@ def tile_multiheadlatentattention_pa_kernel(
             up_w = [w2_codes[("up", g, group)] for g in range(DQ_PASSES)]
             rope_w = [w2_codes[("rope", g, group // 2)] for g in range(DQ_PASSES)]
             shape = [P, 2, GROUP_HEADS, HALF, 2]
+            heads = slice(group * GROUP_HEADS, (group + 1) * GROUP_HEADS)
             for quad in range(J // QUAD):
                 result = outs.tile([P, GROUP_HEADS, QUAD, DH + DR], F32, tag="res", name="result")
                 for jp in range(QUAD // 2):
                     j0 = quad * QUAD + 2 * jp
                     qr = psum.tile([P, BANK], F32, tag="bank", name="qr")
-                    for jl in range(2):
-                        qc = psum.tile([P, BANK], F32, tag="bank", name="qc")
-                        up_projection(qc[:], j0 + jl, up_w, 0, BANK)
-                        nc.scalar.copy(
-                            out=result[:, :, 2 * jp + jl, 0:DH],
-                            in_=qc[:].rearrange("p (h d) -> p h d", h=GROUP_HEADS),
-                        )
                     for jl in range(2):
                         up_projection(
                             qr[:, jl * ROPE_COLS : (jl + 1) * ROPE_COLS],
@@ -257,37 +255,44 @@ def tile_multiheadlatentattention_pa_kernel(
                         in1=odd_part[:].rearrange("p j h i e -> p h j (i e)"),
                         op=ADD,
                     )
-                nc.sync.dma_start(
-                    out=out_rows[
-                        :,
-                        group * GROUP_HEADS : (group + 1) * GROUP_HEADS,
-                        quad * QUAD : (quad + 1) * QUAD,
-                        :,
-                    ],
-                    in_=result[:],
-                )
+                n_quad = group * (J // QUAD) + quad
+                pieces = 2 if n_quad == 0 or n_quad == GROUPS * (J // QUAD) - 1 else 1
+                width = QUAD // pieces
+                for jj in range(QUAD):
+                    qc = psum.tile([P, BANK], F32, tag="bank", name="qc")
+                    up_projection(qc[:], quad * QUAD + jj, up_w, 0, BANK)
+                    nc.scalar.copy(
+                        out=result[:, :, jj, 0:DH],
+                        in_=qc[:].rearrange("p (h d) -> p h d", h=GROUP_HEADS),
+                    )
+                    if jj % 2 == 1:
+                        step = PAIRS + 2 * n_quad + jj // 2
+                        if step < len(stage2_blocks):
+                            quantise_stage2_block(step)
+                    if (jj + 1) % width == 0:
+                        nc.sync.dma_start(
+                            out=out_rows[:, heads, quad * QUAD + jj + 1 - width : quad * QUAD + jj + 1, :],
+                            in_=result[:, :, jj + 1 - width : jj + 1, :],
+                        )
 
         load_x(0)
         load_w_down(0)
         for pair in range(1, PAIRS):
             load_x(pair)
-        load_w_down(1)
-        load_stage2(stage2_order[0])
-
         x_to_codes(0)
-        load_stage2(stage2_order[1])
         for c in range(D_PASSES):
             wd_codes[(c, 0)] = quantise_weight_block(wdq, wd_raw[(c, 0)][:])
+        load_w_down(1)
+        for n in range(3):
+            load_stage2(stage2_order[n])
         for pair in range(PAIRS):
             if pair + 1 < PAIRS:
                 x_to_codes(pair + 1)
-                load_stage2(stage2_order[pair + 2])
+                load_stage2(stage2_order[pair + 3])
             down_projection(0, pair)
             wd_codes[(pair, 1)] = quantise_weight_block(wdq, wd_raw[(pair, 1)][:])
         for pair in range(PAIRS):
             down_projection(1, pair)
-            quantise_group_weights(pair)
-            if pair == 1:
-                load_stage2(stage2_order[5])
+            quantise_stage2_block(pair)
         for group in range(GROUPS):
             head_group(group)

@@ -44,9 +44,9 @@ def tile_multiheadlatentattention_pa_kernel(
         name="wgroup", bufs=3
     ) as wgroup, tc.tile_pool(name="agroup", bufs=2) as agroup, tc.tile_pool(
         name="xq", bufs=J
-    ) as xq, tc.tile_pool(name="wdq", bufs=2 * D_PASSES) as wdq, tc.tile_pool(
+    ) as xq, tc.tile_pool(name="wq", bufs=20) as wq, tc.tile_pool(
         name="dqq", bufs=DQ_PASSES * PAIRS
-    ) as dqq, tc.tile_pool(name="w2q", bufs=12) as w2q, tc.tile_pool(
+    ) as dqq, tc.tile_pool(
         name="parts", bufs=3
     ) as parts, tc.tile_pool(name="outs", bufs=3) as outs, tc.psum_pool(
         name="psum", bufs=8
@@ -69,10 +69,14 @@ def tile_multiheadlatentattention_pa_kernel(
         x_raw = {}
         wd_raw = {}
         w2_raw = {}
+        x_banks = {}
+        x_grouped = {}
         x_codes = {}
-        wd_codes = {}
+        dq_banks = {}
+        dq_grouped = {}
         dq_codes = {}
-        w2_codes = {}
+        w_grouped = []
+        w_codes = {}
 
         def load_x(pair):
             t = raw8.tile([P, 2 * D], BF16, tag="raw8", name="x_raw")
@@ -93,50 +97,64 @@ def tile_multiheadlatentattention_pa_kernel(
                     )
                 wd_raw[(c, half)] = t
 
-        def load_stage2(key):
-            name, g, half = key
+        def load_stage2(name, g, half):
             src = w_up[:, half * 2 * BANK : (half + 1) * 2 * BANK] if name == "up" else w_rope
             t = raw8.tile([P, PACK, 2 * BANK], BF16, tag="raw8", name="w2_raw")
             nc.sync.dma_start(
                 out=t[:], in_=src[g * K_PASS : (g + 1) * K_PASS, :].rearrange("(t p) n -> p t n", p=P)
             )
-            w2_raw[key] = t
+            w2_raw[(name, g, half)] = t
 
-        stage2_order = []
-        for half in range(2):
-            for g in range(DQ_PASSES):
-                stage2_order.append(("up", g, half))
-            if half == 0:
-                for g in range(DQ_PASSES):
-                    stage2_order.append(("rope", g, 0))
+        stage2_loads = (
+            [("up", g, 0) for g in range(DQ_PASSES)]
+            + [("rope", g, 0) for g in range(DQ_PASSES)]
+            + [("up", g, 1) for g in range(DQ_PASSES)]
+        )
 
-        def quantise_weight_block(pool, rows):
+        w_blocks = (
+            [("down", c, half) for half in range(2) for c in range(D_PASSES)]
+            + [("up", g, group) for g in range(DQ_PASSES) for group in range(2)]
+            + [("rope", g, half) for half in range(2) for g in range(DQ_PASSES)]
+            + [("up", g, group) for group in range(2, GROUPS) for g in range(DQ_PASSES)]
+        )
+
+        def block_rows(name, g, part):
+            if name == "down":
+                return wd_raw[(g, part)][:]
+            rows = w2_raw[("up", g, part // 2)] if name == "up" else w2_raw[("rope", g, 0)]
+            return rows[:, :, (part % 2) * BANK : (part % 2 + 1) * BANK]
+
+        def regroup_next_block(vector_cols):
+            name, g, part = w_blocks[len(w_grouped)]
+            rows = block_rows(name, g, part)
             grouped = wgroup.tile([P, BANK, PACK], BF16, align_bytes=64, tag="wg", name="grouped")
-            v = VECTOR_COLS
-            nc.vector.tensor_copy(
-                out=grouped[:, 0:v, :].rearrange("p (c i) t -> p c t i", i=4),
-                in_=rows[:, :, 0:v].rearrange("p t (c i) -> p c t i", i=4),
-            )
-            nc.scalar.copy(
-                out=grouped[:, v:BANK, :].rearrange("p (c i) t -> p c t i", i=4),
-                in_=rows[:, :, v:BANK].rearrange("p t (c i) -> p c t i", i=4),
-            )
-            codes = pool.tile([P, BANK], U32, align_bytes=64, tag="codes", name="codes")
-            scales = pool.tile([P, BANK], U8, align_bytes=64, tag="scales", name="scales")
+            v = vector_cols
+            if v > 0:
+                nc.vector.tensor_copy(
+                    out=grouped[:, 0:v, :].rearrange("p (c i) t -> p c t i", i=4),
+                    in_=rows[:, :, 0:v].rearrange("p t (c i) -> p c t i", i=4),
+                )
+            if v < BANK:
+                nc.scalar.copy(
+                    out=grouped[:, v:BANK, :].rearrange("p (c i) t -> p c t i", i=4),
+                    in_=rows[:, :, v:BANK].rearrange("p t (c i) -> p c t i", i=4),
+                )
+            w_grouped.append(grouped)
+
+        def quantise_next_block():
+            n = len(w_codes)
+            codes = wq.tile([P, BANK], U32, align_bytes=64, tag="codes", name="codes")
+            scales = wq.tile([P, BANK], U8, align_bytes=64, tag="scales", name="scales")
             nc.vector.quantize_mx(
                 out=codes[:].bitcast(FP8X4),
                 scales=scales[:],
-                in_=grouped[:].rearrange("p n t -> p (n t)"),
+                in_=w_grouped[n][:].rearrange("p n t -> p (n t)"),
             )
-            return codes, scales
+            w_codes[w_blocks[n]] = (codes, scales)
 
-        def x_to_codes(pair):
+        def transpose_x(pair):
             words = x_raw[pair][:].bitcast(F32)
             for jl in range(2):
-                grouped = agroup.tile([P, D], BF16, align_bytes=64, tag="xg", name="x_grouped")
-                grouped_words = grouped[:].bitcast(F32).rearrange(
-                    "q (c s u) -> q c s u", c=D_PASSES, u=2
-                )
                 for b in range(2):
                     xt = psum.tile([P, BANK], F32, tag="bank", name="xt")
                     for cl in range(2):
@@ -147,23 +165,33 @@ def tile_multiheadlatentattention_pa_kernel(
                                 words[:, col0 : col0 + P],
                                 ident[:],
                             )
-                    nc.scalar.copy(
-                        out=grouped_words[:, 2 * b : 2 * b + 2, :, :],
-                        in_=xt[:].rearrange("q (c u s) -> q c s u", c=2, u=2),
-                    )
-                codes = xq.tile([P, D_PASSES * P], U32, align_bytes=64, tag="codes", name="x_codes")
-                scales = xq.tile([P, D_PASSES * P], U8, align_bytes=64, tag="scales", name="x_scales")
-                nc.vector.quantize_mx(out=codes[:].bitcast(FP8X4), scales=scales[:], in_=grouped[:])
-                x_codes[2 * pair + jl] = (codes, scales)
+                    x_banks[(pair, jl, b)] = xt
+
+        def copy_x(pair, jl):
+            grouped = agroup.tile([P, D], BF16, align_bytes=64, tag="xg", name="x_grouped")
+            grouped_words = grouped[:].bitcast(F32).rearrange("q (c s u) -> q c s u", c=D_PASSES, u=2)
+            for b in range(2):
+                nc.scalar.copy(
+                    out=grouped_words[:, 2 * b : 2 * b + 2, :, :],
+                    in_=x_banks[(pair, jl, b)][:].rearrange("q (c u s) -> q c s u", c=2, u=2),
+                )
+            x_grouped[(pair, jl)] = grouped
+
+        def quantise_x(pair, jl):
+            codes = xq.tile([P, D_PASSES * P], U32, align_bytes=64, tag="codes", name="x_codes")
+            scales = xq.tile([P, D_PASSES * P], U8, align_bytes=64, tag="scales", name="x_scales")
+            nc.vector.quantize_mx(
+                out=codes[:].bitcast(FP8X4), scales=scales[:], in_=x_grouped[(pair, jl)][:]
+            )
+            x_codes[2 * pair + jl] = (codes, scales)
 
         def down_projection(half, pair):
-            grouped = agroup.tile([P, 2, P, PACK], BF16, align_bytes=64, tag="dqg", name="dq_grouped")
             for jl in range(2):
                 xc, xs = x_codes[2 * pair + jl]
                 acc = psum.tile([P, BANK], F32, tag="bank", name="dq_acc")
                 for t in range(PACK):
                     for c in range(D_PASSES):
-                        wc, ws = wd_codes[(c, half)]
+                        wc, ws = w_codes[("down", c, half)]
                         nc.tensor.matmul_mx(
                             out=acc[:, t * P : (t + 1) * P],
                             lhsT=wc[:, t * P : (t + 1) * P].bitcast(FP8X4),
@@ -173,33 +201,26 @@ def tile_multiheadlatentattention_pa_kernel(
                             start=(c == 0),
                             stop=(c == D_PASSES - 1),
                         )
+                dq_banks[(half, pair, jl)] = acc
+
+        def copy_dq(half, pair):
+            grouped = agroup.tile([P, 2, P, PACK], BF16, align_bytes=64, tag="dqg", name="dq_grouped")
+            for jl in range(2):
                 nc.scalar.copy(
-                    out=grouped[:, jl, :, :], in_=acc[:].rearrange("p (t s) -> p s t", t=PACK)
+                    out=grouped[:, jl, :, :],
+                    in_=dq_banks[(half, pair, jl)][:].rearrange("p (t s) -> p s t", t=PACK),
                 )
+            dq_grouped[(half, pair)] = grouped
+
+        def quantise_dq(half, pair):
             codes = dqq.tile([P, 2 * P], U32, align_bytes=64, tag="codes", name="dq_codes")
             scales = dqq.tile([P, 2 * P], U8, align_bytes=64, tag="scales", name="dq_scales")
             nc.vector.quantize_mx(
                 out=codes[:].bitcast(FP8X4),
                 scales=scales[:],
-                in_=grouped[:].rearrange("p j s t -> p (j s t)"),
+                in_=dq_grouped[(half, pair)][:].rearrange("p j s t -> p (j s t)"),
             )
             dq_codes[(half, pair)] = (codes, scales)
-
-        stage2_blocks = []
-        for group in range(GROUPS):
-            for g in range(DQ_PASSES):
-                stage2_blocks.append(("up", g, group))
-            if group % 2 == 0:
-                for g in range(DQ_PASSES):
-                    stage2_blocks.append(("rope", g, group // 2))
-
-        def quantise_stage2_block(n):
-            name, g, part = stage2_blocks[n]
-            rows = w2_raw[("up", g, part // 2)] if name == "up" else w2_raw[("rope", g, 0)]
-            side = part % 2
-            w2_codes[stage2_blocks[n]] = quantise_weight_block(
-                w2q, rows[:, :, side * BANK : (side + 1) * BANK]
-            )
 
         def up_projection(acc, j, weights, col0, width):
             for g in range(DQ_PASSES):
@@ -216,83 +237,107 @@ def tile_multiheadlatentattention_pa_kernel(
                     stop=(g == DQ_PASSES - 1),
                 )
 
-        def head_group(group):
-            up_w = [w2_codes[("up", g, group)] for g in range(DQ_PASSES)]
-            rope_w = [w2_codes[("rope", g, group // 2)] for g in range(DQ_PASSES)]
+        def quad_of_tokens(group, quad):
+            up_w = [w_codes[("up", g, group)] for g in range(DQ_PASSES)]
+            rope_w = [w_codes[("rope", g, group // 2)] for g in range(DQ_PASSES)]
             shape = [P, 2, GROUP_HEADS, HALF, 2]
             heads = slice(group * GROUP_HEADS, (group + 1) * GROUP_HEADS)
-            for quad in range(J // QUAD):
-                result = outs.tile([P, GROUP_HEADS, QUAD, DH + DR], F32, tag="res", name="result")
-                for jp in range(QUAD // 2):
-                    j0 = quad * QUAD + 2 * jp
-                    qr = psum.tile([P, BANK], F32, tag="bank", name="qr")
-                    for jl in range(2):
-                        up_projection(
-                            qr[:, jl * ROPE_COLS : (jl + 1) * ROPE_COLS],
-                            j0 + jl,
-                            rope_w,
-                            (group % 2) * ROPE_COLS,
-                            ROPE_COLS,
-                        )
-                    pairs = qr[:].rearrange("p (j h i e) -> p j h i e", j=2, h=GROUP_HEADS, e=2)
-                    even_part = parts.tile(shape, F32, tag="even", name="even_part")
-                    odd_part = parts.tile(shape, F32, tag="odd", name="odd_part")
-                    nc.vector.tensor_tensor(
-                        out=even_part[:],
-                        in0=pairs[:, :, :, :, 0:1].to_broadcast(shape),
-                        in1=even_factor[:, j0 : j0 + 2, :, :].unsqueeze(2).to_broadcast(shape),
-                        op=MULT,
+            n_quad = group * (J // QUAD) + quad
+            result = outs.tile([P, GROUP_HEADS, QUAD, DH + DR], F32, tag="res", name="result")
+            for jp in range(QUAD // 2):
+                j0 = quad * QUAD + 2 * jp
+                qr = psum.tile([P, BANK], F32, tag="bank", name="qr")
+                for jl in range(2):
+                    up_projection(
+                        qr[:, jl * ROPE_COLS : (jl + 1) * ROPE_COLS],
+                        j0 + jl,
+                        rope_w,
+                        (group % 2) * ROPE_COLS,
+                        ROPE_COLS,
                     )
-                    nc.vector.tensor_tensor(
-                        out=odd_part[:],
-                        in0=pairs[:, :, :, :, 1:2].to_broadcast(shape),
-                        in1=odd_factor[:, j0 : j0 + 2, :, :].unsqueeze(2).to_broadcast(shape),
-                        op=MULT,
+                pairs = qr[:].rearrange("p (j h i e) -> p j h i e", j=2, h=GROUP_HEADS, e=2)
+                even_part = parts.tile(shape, F32, tag="even", name="even_part")
+                odd_part = parts.tile(shape, F32, tag="odd", name="odd_part")
+                nc.vector.tensor_tensor(
+                    out=even_part[:],
+                    in0=pairs[:, :, :, :, 0:1].to_broadcast(shape),
+                    in1=even_factor[:, j0 : j0 + 2, :, :].unsqueeze(2).to_broadcast(shape),
+                    op=MULT,
+                )
+                nc.vector.tensor_tensor(
+                    out=odd_part[:],
+                    in0=pairs[:, :, :, :, 1:2].to_broadcast(shape),
+                    in1=odd_factor[:, j0 : j0 + 2, :, :].unsqueeze(2).to_broadcast(shape),
+                    op=MULT,
+                )
+                nc.gpsimd.tensor_tensor(
+                    out=result[:, :, 2 * jp : 2 * jp + 2, DH : DH + DR],
+                    in0=even_part[:].rearrange("p j h i e -> p h j (i e)"),
+                    in1=odd_part[:].rearrange("p j h i e -> p h j (i e)"),
+                    op=ADD,
+                )
+            pieces = 2 if n_quad == 0 or n_quad == GROUPS * (J // QUAD) - 1 else 1
+            width = QUAD // pieces
+            for jj in range(QUAD):
+                qc = psum.tile([P, BANK], F32, tag="bank", name="qc")
+                up_projection(qc[:], quad * QUAD + jj, up_w, 0, BANK)
+                nc.scalar.copy(
+                    out=result[:, :, jj, 0:DH],
+                    in_=qc[:].rearrange("p (h d) -> p h d", h=GROUP_HEADS),
+                )
+                if jj == 1 and len(w_codes) < len(w_grouped):
+                    quantise_next_block()
+                if (jj + 1) % width == 0:
+                    nc.sync.dma_start(
+                        out=out_rows[:, heads, quad * QUAD + jj + 1 - width : quad * QUAD + jj + 1, :],
+                        in_=result[:, :, jj + 1 - width : jj + 1, :],
                     )
-                    nc.gpsimd.tensor_tensor(
-                        out=result[:, :, 2 * jp : 2 * jp + 2, DH : DH + DR],
-                        in0=even_part[:].rearrange("p j h i e -> p h j (i e)"),
-                        in1=odd_part[:].rearrange("p j h i e -> p h j (i e)"),
-                        op=ADD,
-                    )
-                n_quad = group * (J // QUAD) + quad
-                pieces = 2 if n_quad == 0 or n_quad == GROUPS * (J // QUAD) - 1 else 1
-                width = QUAD // pieces
-                for jj in range(QUAD):
-                    qc = psum.tile([P, BANK], F32, tag="bank", name="qc")
-                    up_projection(qc[:], quad * QUAD + jj, up_w, 0, BANK)
-                    nc.scalar.copy(
-                        out=result[:, :, jj, 0:DH],
-                        in_=qc[:].rearrange("p (h d) -> p h d", h=GROUP_HEADS),
-                    )
-                    if jj % 2 == 1:
-                        step = PAIRS + 2 * n_quad + jj // 2
-                        if step < len(stage2_blocks):
-                            quantise_stage2_block(step)
-                    if (jj + 1) % width == 0:
-                        nc.sync.dma_start(
-                            out=out_rows[:, heads, quad * QUAD + jj + 1 - width : quad * QUAD + jj + 1, :],
-                            in_=result[:, :, jj + 1 - width : jj + 1, :],
-                        )
+            if len(w_grouped) < len(w_blocks):
+                regroup_next_block(0)
 
-        load_x(0)
-        load_w_down(0)
-        for pair in range(1, PAIRS):
-            load_x(pair)
-        x_to_codes(0)
-        for c in range(D_PASSES):
-            wd_codes[(c, 0)] = quantise_weight_block(wdq, wd_raw[(c, 0)][:])
-        load_w_down(1)
-        for n in range(3):
-            load_stage2(stage2_order[n])
-        for pair in range(PAIRS):
-            if pair + 1 < PAIRS:
-                x_to_codes(pair + 1)
-                load_stage2(stage2_order[pair + 3])
-            down_projection(0, pair)
-            wd_codes[(pair, 1)] = quantise_weight_block(wdq, wd_raw[(pair, 1)][:])
-        for pair in range(PAIRS):
-            down_projection(1, pair)
-            quantise_stage2_block(pair)
-        for group in range(GROUPS):
-            head_group(group)
+        with tc.manual_schedule():
+            load_x(0)
+            load_w_down(0)
+            for pair in range(1, PAIRS):
+                load_x(pair)
+            transpose_x(0)
+            copy_x(0, 0)
+            regroup_next_block(VECTOR_COLS)
+            quantise_x(0, 0)
+            copy_x(0, 1)
+            for c in range(1, D_PASSES):
+                regroup_next_block(VECTOR_COLS)
+                quantise_next_block()
+            load_w_down(1)
+            for n in range(3):
+                load_stage2(*stage2_loads[n])
+            quantise_next_block()
+            quantise_x(0, 1)
+
+            for pair in range(PAIRS):
+                if pair + 1 < PAIRS:
+                    transpose_x(pair + 1)
+                    load_stage2(*stage2_loads[pair + 3])
+                    copy_x(pair + 1, 0)
+                    copy_x(pair + 1, 1)
+                down_projection(0, pair)
+                if pair + 1 < PAIRS:
+                    quantise_x(pair + 1, 0)
+                    quantise_x(pair + 1, 1)
+                copy_dq(0, pair)
+                regroup_next_block(BANK)
+                quantise_dq(0, pair)
+                quantise_next_block()
+
+            for pair in range(PAIRS):
+                down_projection(1, pair)
+                regroup_next_block(VECTOR_COLS)
+                regroup_next_block(VECTOR_COLS)
+                quantise_next_block()
+                copy_dq(1, pair)
+                quantise_dq(1, pair)
+                quantise_next_block()
+
+            for group in range(GROUPS):
+                for quad in range(J // QUAD):
+                    quad_of_tokens(group, quad)

from concourse import mybir
from concourse.masks import make_identity

BF16 = mybir.dt.bfloat16
F32 = mybir.dt.float32
U32 = mybir.dt.uint32
U8 = mybir.dt.uint8
FP8X4 = mybir.dt.float8_e4m3fn_x4
MULT = mybir.AluOpType.mult
ADD = mybir.AluOpType.add

P = 128
PACK = 4
K_PASS = P * PACK
BANK = 512

S, D, DQ = 1024, 2048, 1024
H, DH, DR = 16, 128, 64
HALF = DR // 2
J = S // P
PAIRS = J // 2
D_PASSES = D // K_PASS
DQ_PASSES = DQ // K_PASS
GROUP_HEADS = BANK // DH
GROUPS = H // GROUP_HEADS
ROPE_COLS = GROUP_HEADS * DR
QUAD = 4

VECTOR_COLS = 320

FLOPS = 2 * S * D * DQ + 2 * S * DQ * (H * DH + H * DR)


def tile_multiheadlatentattention_pa_kernel(
    tc, x, w_down, w_up, w_rope, rope_cos, rope_sin, out
):
    nc = tc.nc
    x_rows = x.flatten_outer_dims().rearrange("(p j) d -> p j d", j=J)
    out_rows = out.flatten_outer_dims().rearrange("(h p j) f -> p h j f", h=H, j=J)

    with tc.tile_pool(name="const", bufs=1) as const, tc.tile_pool(
        name="raw8", bufs=6
    ) as raw8, tc.tile_pool(name="raw4", bufs=D_PASSES) as raw4, tc.tile_pool(
        name="wgroup", bufs=3
    ) as wgroup, tc.tile_pool(name="agroup", bufs=2) as agroup, tc.tile_pool(
        name="xq", bufs=J
    ) as xq, tc.tile_pool(name="wq", bufs=20) as wq, tc.tile_pool(
        name="dqq", bufs=DQ_PASSES * PAIRS
    ) as dqq, tc.tile_pool(
        name="parts", bufs=3
    ) as parts, tc.tile_pool(name="outs", bufs=3) as outs, tc.psum_pool(
        name="psum", bufs=8
    ) as psum:
        ident = const.tile([P, P], F32)
        make_identity(nc, ident[:])
        cos_sb = const.tile([P, J, HALF], BF16)
        sin_sb = const.tile([P, J, HALF], BF16)
        nc.scalar.dma_start(out=cos_sb[:], in_=rope_cos.rearrange("(p j) i -> p j i", j=J))
        nc.scalar.dma_start(out=sin_sb[:], in_=rope_sin.rearrange("(p j) i -> p j i", j=J))
        even_factor = const.tile([P, J, HALF, 2], F32)
        odd_factor = const.tile([P, J, HALF, 2], F32)
        nc.gpsimd.tensor_copy(out=even_factor[:, :, :, 0], in_=cos_sb[:])
        nc.gpsimd.tensor_copy(out=even_factor[:, :, :, 1], in_=sin_sb[:])
        nc.gpsimd.tensor_scalar(
            out=odd_factor[:, :, :, 0], in0=sin_sb[:], scalar1=-1.0, scalar2=0.0, op0=MULT, op1=ADD
        )
        nc.gpsimd.tensor_copy(out=odd_factor[:, :, :, 1], in_=cos_sb[:])

        x_raw = {}
        wd_raw = {}
        w2_raw = {}
        x_banks = {}
        x_grouped = {}
        x_codes = {}
        dq_banks = {}
        dq_grouped = {}
        dq_codes = {}
        w_grouped = []
        w_codes = {}

        def load_x(pair):
            t = raw8.tile([P, 2 * D], BF16, tag="raw8", name="x_raw")
            nc.sync.dma_start(
                out=t[:].rearrange("p (j d) -> p j d", j=2), in_=x_rows[:, 2 * pair : 2 * pair + 2, :]
            )
            x_raw[pair] = t

        def load_w_down(half):
            cols = slice(half * BANK, (half + 1) * BANK)
            for c in range(D_PASSES):
                t = raw4.tile([P, PACK, BANK], BF16, tag="raw4", name="wd_raw")
                for u in range(2):
                    row0 = c * K_PASS + u * 2 * P
                    nc.sync.dma_start(
                        out=t[:, 2 * u : 2 * u + 2, :],
                        in_=w_down[row0 : row0 + 2 * P, cols].rearrange("(q e) n -> q e n", e=2),
                    )
                wd_raw[(c, half)] = t

        def load_stage2(name, g, half):
            src = w_up[:, half * 2 * BANK : (half + 1) * 2 * BANK] if name == "up" else w_rope
            t = raw8.tile([P, PACK, 2 * BANK], BF16, tag="raw8", name="w2_raw")
            nc.sync.dma_start(
                out=t[:], in_=src[g * K_PASS : (g + 1) * K_PASS, :].rearrange("(t p) n -> p t n", p=P)
            )
            w2_raw[(name, g, half)] = t

        stage2_loads = (
            [("up", g, 0) for g in range(DQ_PASSES)]
            + [("rope", g, 0) for g in range(DQ_PASSES)]
            + [("up", g, 1) for g in range(DQ_PASSES)]
        )

        w_blocks = (
            [("down", c, half) for half in range(2) for c in range(D_PASSES)]
            + [("up", g, group) for g in range(DQ_PASSES) for group in range(2)]
            + [("rope", g, half) for half in range(2) for g in range(DQ_PASSES)]
            + [("up", g, group) for group in range(2, GROUPS) for g in range(DQ_PASSES)]
        )

        def block_rows(name, g, part):
            if name == "down":
                return wd_raw[(g, part)][:]
            rows = w2_raw[("up", g, part // 2)] if name == "up" else w2_raw[("rope", g, 0)]
            return rows[:, :, (part % 2) * BANK : (part % 2 + 1) * BANK]

        def regroup_next_block(vector_cols):
            name, g, part = w_blocks[len(w_grouped)]
            rows = block_rows(name, g, part)
            grouped = wgroup.tile([P, BANK, PACK], BF16, align_bytes=64, tag="wg", name="grouped")
            v = vector_cols
            if v > 0:
                nc.vector.tensor_copy(
                    out=grouped[:, 0:v, :].rearrange("p (c i) t -> p c t i", i=4),
                    in_=rows[:, :, 0:v].rearrange("p t (c i) -> p c t i", i=4),
                )
            if v < BANK:
                nc.scalar.copy(
                    out=grouped[:, v:BANK, :].rearrange("p (c i) t -> p c t i", i=4),
                    in_=rows[:, :, v:BANK].rearrange("p t (c i) -> p c t i", i=4),
                )
            w_grouped.append(grouped)

        def quantise_next_block():
            n = len(w_codes)
            codes = wq.tile([P, BANK], U32, align_bytes=64, tag="codes", name="codes")
            scales = wq.tile([P, BANK], U8, align_bytes=64, tag="scales", name="scales")
            nc.vector.quantize_mx(
                out=codes[:].bitcast(FP8X4),
                scales=scales[:],
                in_=w_grouped[n][:].rearrange("p n t -> p (n t)"),
            )
            w_codes[w_blocks[n]] = (codes, scales)

        def transpose_x(pair):
            words = x_raw[pair][:].bitcast(F32)
            for jl in range(2):
                for b in range(2):
                    xt = psum.tile([P, BANK], F32, tag="bank", name="xt")
                    for cl in range(2):
                        for u in range(2):
                            col0 = jl * (D // 2) + (2 * b + cl) * 2 * P + u * P
                            nc.tensor.transpose(
                                xt[:, (2 * cl + u) * P : (2 * cl + u + 1) * P],
                                words[:, col0 : col0 + P],
                                ident[:],
                            )
                    x_banks[(pair, jl, b)] = xt

        def copy_x(pair, jl):
            grouped = agroup.tile([P, D], BF16, align_bytes=64, tag="xg", name="x_grouped")
            grouped_words = grouped[:].bitcast(F32).rearrange("q (c s u) -> q c s u", c=D_PASSES, u=2)
            for b in range(2):
                nc.scalar.copy(
                    out=grouped_words[:, 2 * b : 2 * b + 2, :, :],
                    in_=x_banks[(pair, jl, b)][:].rearrange("q (c u s) -> q c s u", c=2, u=2),
                )
            x_grouped[(pair, jl)] = grouped

        def quantise_x(pair, jl):
            codes = xq.tile([P, D_PASSES * P], U32, align_bytes=64, tag="codes", name="x_codes")
            scales = xq.tile([P, D_PASSES * P], U8, align_bytes=64, tag="scales", name="x_scales")
            nc.vector.quantize_mx(
                out=codes[:].bitcast(FP8X4), scales=scales[:], in_=x_grouped[(pair, jl)][:]
            )
            x_codes[2 * pair + jl] = (codes, scales)

        def down_projection(half, pair):
            for jl in range(2):
                xc, xs = x_codes[2 * pair + jl]
                acc = psum.tile([P, BANK], F32, tag="bank", name="dq_acc")
                for t in range(PACK):
                    for c in range(D_PASSES):
                        wc, ws = w_codes[("down", c, half)]
                        nc.tensor.matmul_mx(
                            out=acc[:, t * P : (t + 1) * P],
                            lhsT=wc[:, t * P : (t + 1) * P].bitcast(FP8X4),
                            lhsT_scale=ws[:, t * P : (t + 1) * P],
                            rhs=xc[:, c * P : (c + 1) * P].bitcast(FP8X4),
                            rhs_scale=xs[:, c * P : (c + 1) * P],
                            start=(c == 0),
                            stop=(c == D_PASSES - 1),
                        )
                dq_banks[(half, pair, jl)] = acc

        def copy_dq(half, pair):
            grouped = agroup.tile([P, 2, P, PACK], BF16, align_bytes=64, tag="dqg", name="dq_grouped")
            for jl in range(2):
                nc.scalar.copy(
                    out=grouped[:, jl, :, :],
                    in_=dq_banks[(half, pair, jl)][:].rearrange("p (t s) -> p s t", t=PACK),
                )
            dq_grouped[(half, pair)] = grouped

        def quantise_dq(half, pair):
            codes = dqq.tile([P, 2 * P], U32, align_bytes=64, tag="codes", name="dq_codes")
            scales = dqq.tile([P, 2 * P], U8, align_bytes=64, tag="scales", name="dq_scales")
            nc.vector.quantize_mx(
                out=codes[:].bitcast(FP8X4),
                scales=scales[:],
                in_=dq_grouped[(half, pair)][:].rearrange("p j s t -> p (j s t)"),
            )
            dq_codes[(half, pair)] = (codes, scales)

        def up_projection(acc, j, weights, col0, width):
            for g in range(DQ_PASSES):
                ac, asc = dq_codes[(g, j // 2)]
                wc, ws = weights[g]
                tok = slice((j % 2) * P, (j % 2 + 1) * P)
                nc.tensor.matmul_mx(
                    out=acc,
                    lhsT=ac[:, tok].bitcast(FP8X4),
                    lhsT_scale=asc[:, tok],
                    rhs=wc[:, col0 : col0 + width].bitcast(FP8X4),
                    rhs_scale=ws[:, col0 : col0 + width],
                    start=(g == 0),
                    stop=(g == DQ_PASSES - 1),
                )

        def quad_of_tokens(group, quad):
            up_w = [w_codes[("up", g, group)] for g in range(DQ_PASSES)]
            rope_w = [w_codes[("rope", g, group // 2)] for g in range(DQ_PASSES)]
            shape = [P, 2, GROUP_HEADS, HALF, 2]
            heads = slice(group * GROUP_HEADS, (group + 1) * GROUP_HEADS)
            n_quad = group * (J // QUAD) + quad
            result = outs.tile([P, GROUP_HEADS, QUAD, DH + DR], F32, tag="res", name="result")
            for jp in range(QUAD // 2):
                j0 = quad * QUAD + 2 * jp
                qr = psum.tile([P, BANK], F32, tag="bank", name="qr")
                for jl in range(2):
                    up_projection(
                        qr[:, jl * ROPE_COLS : (jl + 1) * ROPE_COLS],
                        j0 + jl,
                        rope_w,
                        (group % 2) * ROPE_COLS,
                        ROPE_COLS,
                    )
                pairs = qr[:].rearrange("p (j h i e) -> p j h i e", j=2, h=GROUP_HEADS, e=2)
                even_part = parts.tile(shape, F32, tag="even", name="even_part")
                odd_part = parts.tile(shape, F32, tag="odd", name="odd_part")
                nc.vector.tensor_tensor(
                    out=even_part[:],
                    in0=pairs[:, :, :, :, 0:1].to_broadcast(shape),
                    in1=even_factor[:, j0 : j0 + 2, :, :].unsqueeze(2).to_broadcast(shape),
                    op=MULT,
                )
                nc.vector.tensor_tensor(
                    out=odd_part[:],
                    in0=pairs[:, :, :, :, 1:2].to_broadcast(shape),
                    in1=odd_factor[:, j0 : j0 + 2, :, :].unsqueeze(2).to_broadcast(shape),
                    op=MULT,
                )
                nc.gpsimd.tensor_tensor(
                    out=result[:, :, 2 * jp : 2 * jp + 2, DH : DH + DR],
                    in0=even_part[:].rearrange("p j h i e -> p h j (i e)"),
                    in1=odd_part[:].rearrange("p j h i e -> p h j (i e)"),
                    op=ADD,
                )
            pieces = 2 if n_quad == 0 or n_quad == GROUPS * (J // QUAD) - 1 else 1
            width = QUAD // pieces
            for jj in range(QUAD):
                qc = psum.tile([P, BANK], F32, tag="bank", name="qc")
                up_projection(qc[:], quad * QUAD + jj, up_w, 0, BANK)
                nc.scalar.copy(
                    out=result[:, :, jj, 0:DH],
                    in_=qc[:].rearrange("p (h d) -> p h d", h=GROUP_HEADS),
                )
                if jj == 1 and len(w_codes) < len(w_grouped):
                    quantise_next_block()
                if (jj + 1) % width == 0:
                    nc.sync.dma_start(
                        out=out_rows[:, heads, quad * QUAD + jj + 1 - width : quad * QUAD + jj + 1, :],
                        in_=result[:, :, jj + 1 - width : jj + 1, :],
                    )
            if len(w_grouped) < len(w_blocks):
                regroup_next_block(0)

        with tc.manual_schedule():
            load_x(0)
            load_w_down(0)
            for pair in range(1, PAIRS):
                load_x(pair)
            transpose_x(0)
            copy_x(0, 0)
            regroup_next_block(VECTOR_COLS)
            quantise_x(0, 0)
            copy_x(0, 1)
            for c in range(1, D_PASSES):
                regroup_next_block(VECTOR_COLS)
                quantise_next_block()
            load_w_down(1)
            for n in range(3):
                load_stage2(*stage2_loads[n])
            quantise_next_block()
            quantise_x(0, 1)

            for pair in range(PAIRS):
                if pair + 1 < PAIRS:
                    transpose_x(pair + 1)
                    load_stage2(*stage2_loads[pair + 3])
                    copy_x(pair + 1, 0)
                    copy_x(pair + 1, 1)
                down_projection(0, pair)
                if pair + 1 < PAIRS:
                    quantise_x(pair + 1, 0)
                    quantise_x(pair + 1, 1)
                copy_dq(0, pair)
                regroup_next_block(BANK)
                quantise_dq(0, pair)
                quantise_next_block()

            for pair in range(PAIRS):
                down_projection(1, pair)
                regroup_next_block(VECTOR_COLS)
                regroup_next_block(VECTOR_COLS)
                quantise_next_block()
                copy_dq(1, pair)
                quantise_dq(1, pair)
                quantise_next_block()

            for group in range(GROUPS):
                for quad in range(J // QUAD):
                    quad_of_tokens(group, quad)
